import numpy as np
import ml_dtypes


def mxq(x, axis, fmt="e4m3"):
    dtype, down = {"e4m3": (ml_dtypes.float8_e4m3fn, 7), "e5m2": (ml_dtypes.float8_e5m2, 14)}[fmt]
    v = np.moveaxis(np.asarray(x, np.float32).astype(ml_dtypes.bfloat16).astype(np.float64), axis, -1)
    blocks = v.reshape(v.shape[:-1] + (-1, 32))
    amax = np.abs(blocks).max(-1, keepdims=True)
    byte = np.maximum(np.where(amax > 0, np.frexp(amax)[1] - 1 + 127, 0) - down, 1)
    scale = np.exp2(byte - 127.0)
    codes = (blocks / scale).astype(np.float32).astype(dtype).astype(np.float64)
    return np.moveaxis((codes * scale).reshape(v.shape), -1, axis)


WIDE = False


def mx_kscale(k):
    if not WIDE:
        return np.ones(k)
    levels = np.array([10, -10, 5, -5, 0])
    if k % 512:
        return np.exp2(np.random.permutation(np.resize(levels, k // 32))).repeat(32)
    a = np.empty((k // 512, 16))
    for p in range(k // 512):
        a[p, :8] = np.random.permutation(np.resize(levels, 8))
        for g in range(8):
            far = levels[np.abs(levels - a[p, g]) >= 10]
            a[p, g + 8] = far[np.random.randint(len(far))]
    return np.exp2(a.ravel()).repeat(32)


BF16 = ml_dtypes.bfloat16


def bf(x):
    return np.asarray(x, np.float32).astype(BF16)


def f64(x):
    return np.asarray(x).astype(np.float64)


N, C, E, T, H, CK = 3, 512, 256, 4096, 8, 64
EPS = 1e-5


def setup_inputs():
    s = mx_kscale(C)
    return {
        "h_attn": bf(np.random.standard_normal((N, T, C)) * 0.4 * s),
        "x": bf(np.random.standard_normal((N, E, T))),
        "masks": bf(np.random.uniform(0.2, 1.0, (N, 1, T))),
        "Wo": bf(np.random.standard_normal((E, C)) * 2.0 / np.sqrt(C) / s[None, :]),
        "bo": bf(np.random.standard_normal(E) * 0.5),
    }


def reference(h_attn, x, masks, Wo, bo):
    o = (mxq(f64(h_attn), 2, "e4m3") @ mxq(f64(Wo), 1, "e4m3").T) + f64(bo)
    y = o.transpose(0, 2, 1) * f64(masks) + f64(x)
    mean = y.mean(-1, keepdims=True)
    var = np.square(y - mean).mean(-1, keepdims=True)
    return (y - mean) / np.sqrt(var + EPS)

@@ -1,0 +1,310 @@
+from contextlib import ExitStack
+
+import concourse.mybir as mybir
+from concourse.masks import make_identity
+
+F32 = mybir.dt.float32
+BF16 = mybir.dt.bfloat16
+U32 = mybir.dt.uint32
+U8 = mybir.dt.uint8
+FP8X4 = mybir.dt.float8_e4m3fn_x4
+ALU = mybir.AluOpType
+ACT = mybir.ActivationFunctionType
+
+P = 128
+SEQS, FRAMES, C_IN, C_OUT = 3, 4096, 512, 256
+EPS = 1e-5
+ROOT_SCALE = FRAMES**-0.5
+FLOPS = 2 * SEQS * FRAMES * C_IN * C_OUT
+
+WORDS = C_IN // 2
+BLOCK = 512
+ROWS = BLOCK // P
+CHUNK = 2 * BLOCK
+CHUNKS_PER_SEQ = FRAMES // CHUNK
+CHUNKS = SEQS * CHUNKS_PER_SEQ
+HALVES = C_OUT // P
+NORM_PART = 2 * CHUNK
+
+LAG = 2
+LOAD_AHEAD = 6
+FLIP_AHEAD = 2
+SPREAD_AHEAD = 1
+MULTIPLY_AHEAD = 1
+SQUARES_BEHIND = 1
+NORM_BEHIND = CHUNKS_PER_SEQ + 1
+RESIDUAL_AHEAD = 5
+
+NORM_VECTOR_COLS = 3 * NORM_PART // 8
+NORM_VECTOR_COLS_END = 21 * NORM_PART // 32
+
+
+def tile_transformerencoderblock_pa_t_kernel(tc, h_attn, x, masks, Wo, bo, out):
+    nc = tc.nc
+    with ExitStack() as ctx:
+        const = ctx.enter_context(tc.tile_pool(name="const", bufs=1))
+        blocks_in = ctx.enter_context(tc.tile_pool(name="blocks_in", bufs=2 * (LOAD_AHEAD - FLIP_AHEAD)))
+        stage = ctx.enter_context(tc.tile_pool(name="stage", bufs=4))
+        per_chunk = ctx.enter_context(tc.tile_pool(name="per_chunk", bufs=FLIP_AHEAD + LAG))
+        per_group = ctx.enter_context(tc.tile_pool(name="per_group", bufs=4))
+        psum = ctx.enter_context(tc.psum_pool(name="psum", bufs=1))
+        ctx.enter_context(tc.manual_schedule())
+
+        ident_f32 = const.tile([P, P], F32)
+        make_identity(nc, ident_f32[:])
+        minus_half = const.tile([P, 1], F32)
+        nc.gpsimd.memset(minus_half[:], -0.5)
+
+        raw, grouped = {}, {}
+        codes, scales, mask_rows = {}, {}, {}
+        product = {}
+        residual, y, sums, pivot, neg_mean, base, rstd, shift = {}, {}, {}, {}, {}, {}, {}, {}
+
+        def flip_two(rows_words, grouped_words, by_vector):
+            bank = psum.tile([P, 2, 2, P], F32, tag="flip", bufs=3)
+            for row_block in range(2):
+                for odd in range(2):
+                    words = rows_words[:, WORDS * row_block + odd : WORDS * (row_block + 1) : 2]
+                    nc.tensor.transpose(bank[:, row_block, odd, :], words, ident_f32[:])
+            dst = grouped_words.rearrange("w (b r u) -> w b r u", b=2, u=2)
+            src = bank[:].rearrange("w b u r -> w b r u")
+            if by_vector:
+                nc.vector.tensor_copy(out=dst, in_=src)
+            else:
+                nc.scalar.copy(out=dst, in_=src)
+
+        small_rows = const.tile([P, 2 * P], BF16)
+        nc.vector.memset(small_rows[:], 0.0)
+        mask_row_count = SEQS * FRAMES // (2 * P)
+        nc.scalar.dma_start(
+            out=small_rows[0:mask_row_count, :], in_=masks.rearrange("n o (i r) -> (n o i) r", r=2 * P)
+        )
+        nc.scalar.dma_start(
+            out=small_rows[mask_row_count : mask_row_count + 1, :], in_=bo.rearrange("(o c) -> o c", o=1)
+        )
+        w_raw = const.tile([P, HALVES * C_IN], BF16)
+        nc.scalar.dma_start(out=w_raw[:], in_=Wo.rearrange("(p h) k -> p (h k)", h=HALVES))
+        mask_words = const.tile([P, mask_row_count], F32)
+        bias_cols = const.tile([P, HALVES], F32)
+        w_grouped = const.tile([P, HALVES * C_IN], BF16, align_bytes=64)
+        w_codes = const.tile([P, C_OUT], U32, align_bytes=64)
+        w_scales = const.tile([P, C_OUT], U8, align_bytes=64)
+
+        def prepare_small_inputs():
+            small_cols = psum.tile([P, CHUNK // 2], F32, tag="spread", bufs=1)
+            nc.tensor.transpose(small_cols[:, 0:P], small_rows[:].bitcast(F32), ident_f32[:])
+            nc.vector.tensor_copy(out=mask_words[:], in_=small_cols[:, 0:mask_row_count])
+            nc.vector.tensor_copy(
+                out=bias_cols[:], in_=small_cols[:, mask_row_count : mask_row_count + 1].bitcast(BF16)
+            )
+            flip_two(w_raw[:].bitcast(F32), w_grouped[:].bitcast(F32), True)
+            nc.vector.quantize_mx(out=w_codes[:].bitcast(FP8X4), scales=w_scales[:], in_=w_grouped[:])
+
+        x_halves = x.rearrange("n (p h) t -> n h p t", h=HALVES)
+        out_halves = out.rearrange("n (p h) t -> n h p t", h=HALVES)
+
+        def load_chunk(chunk):
+            seq, j = divmod(chunk, CHUNKS_PER_SEQ)
+            for i in range(CHUNK // BLOCK):
+                first = CHUNK * j + BLOCK * i
+                raw[(chunk, i)] = blocks_in.tile([P, ROWS * C_IN], BF16, name="raw")
+                nc.sync.dma_start(
+                    out=raw[(chunk, i)][:],
+                    in_=h_attn[seq, first : first + BLOCK, :].rearrange("(p a) k -> p (a k)", a=ROWS),
+                )
+
+        def load_residual(seq, half):
+            group = (seq, half)
+            residual[group] = per_group.tile([P, FRAMES], BF16, name="residual")
+            nc.sync.dma_start(out=residual[group][:], in_=x_halves[seq, half])
+
+        def flip_chunk(chunk, vector_helps):
+            for i in range(CHUNK // BLOCK):
+                grouped[(chunk, i)] = stage.tile([P, 4 * BLOCK], BF16, name="grouped", align_bytes=64)
+                raw_words = raw[(chunk, i)][:].bitcast(F32)
+                grouped_words = grouped[(chunk, i)][:].bitcast(F32)
+                for pair in range(ROWS // 2):
+                    cols = slice(2 * WORDS * pair, 2 * WORDS * (pair + 1))
+                    flip_two(raw_words[:, cols], grouped_words[:, cols], vector_helps and pair == 1)
+
+        def spread_mask(chunk):
+            mask_rows[chunk] = per_chunk.tile([P, CHUNK], BF16, name="mask_rows")
+            spread = psum.tile([P, CHUNK // 2], F32, tag="spread", bufs=1)
+            for i in range(CHUNK // (2 * P)):
+                col = CHUNK // (2 * P) * chunk + i
+                nc.tensor.transpose(
+                    spread[:, P * i : P * (i + 1)],
+                    mask_words[:, col : col + 1].to_broadcast([P, P]),
+                    ident_f32[:],
+                )
+            nc.scalar.copy(out=mask_rows[chunk][:], in_=spread[:].bitcast(BF16))
+
+        def quantise_block(chunk, i):
+            if i == 0:
+                codes[chunk] = per_chunk.tile([P, CHUNK], U32, name="codes", align_bytes=64)
+                scales[chunk] = per_chunk.tile([P, CHUNK], U8, name="scales", align_bytes=64)
+            cols = slice(BLOCK * i, BLOCK * (i + 1))
+            nc.vector.quantize_mx(
+                out=codes[chunk][:, cols].bitcast(FP8X4),
+                scales=scales[chunk][:, cols],
+                in_=grouped[(chunk, i)][:],
+            )
+
+        def multiply(chunk, half):
+            for i in range(CHUNK // BLOCK):
+                cols = slice(BLOCK * i, BLOCK * (i + 1))
+                product[(chunk, half, i)] = psum.tile([P, BLOCK], F32, tag="product", bufs=4, name="product")
+                nc.tensor.matmul_mx(
+                    out=product[(chunk, half, i)][:],
+                    lhsT=w_codes[:, P * half : P * (half + 1)].bitcast(FP8X4),
+                    lhsT_scale=w_scales[:, P * half : P * (half + 1)],
+                    rhs=codes[chunk][:, cols].bitcast(FP8X4),
+                    rhs_scale=scales[chunk][:, cols],
+                    start=True,
+                    stop=True,
+                )
+
+        def add_bias_and_mask(chunk, half):
+            seq, j = divmod(chunk, CHUNKS_PER_SEQ)
+            group = (seq, half)
+            if j == 0:
+                y[group] = per_group.tile([P, FRAMES], F32, name="y")
+                sums[group] = per_group.tile([P, 2, 8], F32, name="sums")
+            for i in range(CHUNK // BLOCK):
+                cols = slice(BLOCK * i, BLOCK * (i + 1))
+                first = CHUNK * j + BLOCK * i
+                nc.vector.scalar_tensor_tensor(
+                    out=y[group][:, first : first + BLOCK].rearrange("e (p a) -> e p a", a=ROWS),
+                    in0=product[(chunk, half, i)][:].rearrange("e (a p) -> e p a", a=ROWS),
+                    scalar=bias_cols[:, half : half + 1],
+                    in1=mask_rows[chunk][:, cols].rearrange("e (p a) -> e p a", a=ROWS),
+                    op0=ALU.add,
+                    op1=ALU.mult,
+                )
+
+        def add_residual(chunk, half):
+            seq, j = divmod(chunk, CHUNKS_PER_SEQ)
+            group = (seq, half)
+            cols = slice(CHUNK * j, CHUNK * (j + 1))
+            nc.vector.scalar_tensor_tensor(
+                out=y[group][:, cols],
+                in0=y[group][:, cols],
+                scalar=1.0,
+                in1=residual[group][:, cols],
+                op0=ALU.mult,
+                op1=ALU.add,
+                accum_out=sums[group][:, 0, j : j + 1],
+            )
+            if j == 0:
+                pivot[group] = per_group.tile([P, 2], F32, name="pivot")
+                for col, factor in enumerate((-1.0 / CHUNK, -ROOT_SCALE / CHUNK)):
+                    nc.gpsimd.tensor_scalar(
+                        out=pivot[group][:, col : col + 1], in0=sums[group][:, 0, 0:1],
+                        scalar1=factor, scalar2=0.0, op0=ALU.mult, op1=ALU.add,
+                    )
+            if j == CHUNKS_PER_SEQ - 1:
+                early_statistics(group)
+
+        def sum_squares(chunk, half):
+            seq, j = divmod(chunk, CHUNKS_PER_SEQ)
+            group = (seq, half)
+            squares = stage.tile([P, CHUNK], BF16, name="squares")
+            nc.scalar.activation(
+                out=squares[:], in_=y[group][:, CHUNK * j : CHUNK * (j + 1)], func=ACT.Square,
+                bias=pivot[group][:, 1:2], scale=ROOT_SCALE, accum_out=sums[group][:, 1, j : j + 1],
+            )
+            if j == CHUNKS_PER_SEQ - 1:
+                late_statistics(group)
+
+        def add_columns(total, row, count):
+            nc.gpsimd.tensor_tensor(out=total, in0=row[:, 0:1], in1=row[:, 1:2], op=ALU.add)
+            for col in range(2, count):
+                nc.gpsimd.tensor_tensor(out=total, in0=total, in1=row[:, col : col + 1], op=ALU.add)
+
+        def early_statistics(group):
+            total = per_group.tile([P, 1], F32, name="total")
+            add_columns(total[:], sums[group][:, 0, :], CHUNKS_PER_SEQ)
+            neg_mean[group] = per_group.tile([P, 1], F32, name="neg_mean")
+            nc.gpsimd.tensor_scalar(
+                out=neg_mean[group][:], in0=total[:],
+                scalar1=-1.0 / FRAMES, scalar2=0.0, op0=ALU.mult, op1=ALU.add,
+            )
+            off = per_group.tile([P, 1], F32, name="off")
+            nc.gpsimd.tensor_tensor(
+                out=off[:], in0=neg_mean[group][:], in1=pivot[group][:, 0:1], op=ALU.subtract
+            )
+            off_sq = per_group.tile([P, 1], F32, name="off_sq")
+            nc.gpsimd.tensor_tensor(out=off_sq[:], in0=off[:], in1=off[:], op=ALU.mult)
+            rest = per_group.tile([P, 1], F32, name="rest")
+            nc.gpsimd.tensor_scalar(
+                out=rest[:], in0=off_sq[:], scalar1=-1.0, scalar2=EPS, op0=ALU.mult, op1=ALU.add
+            )
+            first_squares = per_group.tile([P, 1], F32, name="first_squares")
+            add_columns(first_squares[:], sums[group][:, 1, :], CHUNKS_PER_SEQ - 1)
+            base[group] = per_group.tile([P, 1], F32, name="base")
+            nc.gpsimd.tensor_tensor(out=base[group][:], in0=first_squares[:], in1=rest[:], op=ALU.add)
+
+        def late_statistics(group):
+            var_eps = per_group.tile([P, 1], F32, name="var_eps")
+            nc.gpsimd.tensor_tensor(
+                out=var_eps[:], in0=base[group][:],
+                in1=sums[group][:, 1, CHUNKS_PER_SEQ - 1 : CHUNKS_PER_SEQ], op=ALU.add,
+            )
+            rstd[group] = per_group.tile([P, 1], F32, name="rstd")
+            nc.gpsimd.tensor_tensor(out=rstd[group][:], in0=var_eps[:], in1=minus_half[:], op=ALU.pow)
+            shift[group] = per_group.tile([P, 1], F32, name="shift")
+            nc.gpsimd.tensor_tensor(
+                out=shift[group][:], in0=neg_mean[group][:], in1=rstd[group][:], op=ALU.mult
+            )
+
+        def normalise_and_store(seq, half, part, vector_cols):
+            group = (seq, half)
+            first, last = NORM_PART * part, NORM_PART * (part + 1)
+            split = first + vector_cols
+            nc.vector.tensor_scalar(
+                out=y[group][:, first:split], in0=y[group][:, first:split],
+                scalar1=rstd[group][:, 0:1], scalar2=shift[group][:, 0:1], op0=ALU.mult, op1=ALU.add,
+            )
+            nc.scalar.activation(
+                out=y[group][:, split:last], in_=y[group][:, split:last], func=ACT.Identity,
+                bias=shift[group][:, 0:1], scale=rstd[group][:, 0:1],
+            )
+            nc.sync.dma_start(
+                out=out_halves[seq, half, :, first:last], in_=y[group][:, first:last]
+            )
+
+        def live(chunk):
+            return 0 <= chunk < CHUNKS
+
+        for r in range(-LOAD_AHEAD, CHUNKS + LAG + NORM_BEHIND - CHUNKS_PER_SEQ + FRAMES // NORM_PART):
+            if live(r + FLIP_AHEAD):
+                flip_chunk(r + FLIP_AHEAD, r < 0)
+            if r == -SPREAD_AHEAD:
+                prepare_small_inputs()
+            if live(r + SPREAD_AHEAD):
+                spread_mask(r + SPREAD_AHEAD)
+            if live(r + LOAD_AHEAD):
+                load_chunk(r + LOAD_AHEAD)
+            for half in range(HALVES):
+                if live(r - LAG * half):
+                    add_bias_and_mask(r - LAG * half, half)
+            for half in range(HALVES):
+                if live(r - LAG * half + MULTIPLY_AHEAD):
+                    multiply(r - LAG * half + MULTIPLY_AHEAD, half)
+            for half in range(HALVES):
+                if live(r - LAG * half - SQUARES_BEHIND):
+                    sum_squares(r - LAG * half - SQUARES_BEHIND, half)
+            for half in range(HALVES):
+                if live(r + FLIP_AHEAD):
+                    quantise_block(r + FLIP_AHEAD, half)
+                if live(r - LAG * half):
+                    add_residual(r - LAG * half, half)
+            for half in range(HALVES):
+                seq, part = divmod(r - LAG * half - NORM_BEHIND, CHUNKS_PER_SEQ)
+                if 0 <= seq < SEQS and part < FRAMES // NORM_PART:
+                    busy = r < CHUNKS + LAG
+                    normalise_and_store(seq, half, part, NORM_VECTOR_COLS if busy else NORM_VECTOR_COLS_END)
+            for half in range(HALVES):
+                seq, j = divmod(r - LAG * half + RESIDUAL_AHEAD, CHUNKS_PER_SEQ)
+                if 0 <= seq < SEQS and j == 0:
+                    load_residual(seq, half)

@@ -14,7 +14,6 @@ ACT = mybir.ActivationFunctionType
 P = 128
 SEQS, FRAMES, C_IN, C_OUT = 3, 4096, 512, 256
 EPS = 1e-5
-ROOT_SCALE = FRAMES**-0.5
 FLOPS = 2 * SEQS * FRAMES * C_IN * C_OUT
 
 WORDS = C_IN // 2
@@ -35,7 +34,7 @@ SQUARES_BEHIND = 1
 NORM_BEHIND = CHUNKS_PER_SEQ + 1
 RESIDUAL_AHEAD = 5
 
-NORM_VECTOR_COLS = 3 * NORM_PART // 8
+NORM_VECTOR_COLS = NORM_PART // 2
 NORM_VECTOR_COLS_END = 21 * NORM_PART // 32
 
 
@@ -52,13 +51,23 @@ def tile_transformerencoderblock_pa_t_kernel(tc, h_attn, x, masks, Wo, bo, out):
 
         ident_f32 = const.tile([P, P], F32)
         make_identity(nc, ident_f32[:])
-        minus_half = const.tile([P, 1], F32)
-        nc.gpsimd.memset(minus_half[:], -0.5)
+        one = const.tile([P, 2], F32)
+        nc.vector.memset(one[:], 1.0)
+        nc.scalar.activation(out=one[:, 1:2], in_=one[:, 0:1], func=ACT.Abs_reciprocal_sqrt)
 
         raw, grouped = {}, {}
         codes, scales, mask_rows = {}, {}, {}
         product = {}
-        residual, y, sums, pivot, neg_mean, base, rstd, shift = {}, {}, {}, {}, {}, {}, {}, {}
+        residual, y, sums, neg_pivot, neg_mean, off_sq, rstd, shift = {}, {}, {}, {}, {}, {}, {}, {}
+        chores = []
+
+        def do_chore():
+            if chores:
+                chores.pop(0)()
+
+        def do_chores():
+            while chores:
+                do_chore()
 
         def flip_two(rows_words, grouped_words, by_vector):
             bank = psum.tile([P, 2, 2, P], F32, tag="flip", bufs=3)
@@ -72,6 +81,7 @@ def tile_transformerencoderblock_pa_t_kernel(tc, h_attn, x, masks, Wo, bo, out):
                 nc.vector.tensor_copy(out=dst, in_=src)
             else:
                 nc.scalar.copy(out=dst, in_=src)
+                do_chore()
 
         small_rows = const.tile([P, 2 * P], BF16)
         nc.vector.memset(small_rows[:], 0.0)
@@ -138,6 +148,7 @@ def tile_transformerencoderblock_pa_t_kernel(tc, h_attn, x, masks, Wo, bo, out):
                     ident_f32[:],
                 )
             nc.scalar.copy(out=mask_rows[chunk][:], in_=spread[:].bitcast(BF16))
+            do_chore()
 
         def quantise_block(chunk, i):
             if i == 0:
@@ -196,74 +207,78 @@ def tile_transformerencoderblock_pa_t_kernel(tc, h_attn, x, masks, Wo, bo, out):
                 accum_out=sums[group][:, 0, j : j + 1],
             )
             if j == 0:
-                pivot[group] = per_group.tile([P, 2], F32, name="pivot")
-                for col, factor in enumerate((-1.0 / CHUNK, -ROOT_SCALE / CHUNK)):
-                    nc.gpsimd.tensor_scalar(
-                        out=pivot[group][:, col : col + 1], in0=sums[group][:, 0, 0:1],
-                        scalar1=factor, scalar2=0.0, op0=ALU.mult, op1=ALU.add,
+                neg_pivot[group] = per_group.tile([P, 1], F32, name="neg_pivot")
+                chores.append(
+                    lambda: nc.scalar.activation(
+                        out=neg_pivot[group][:], in_=sums[group][:, 0, 0:1], func=ACT.Identity, scale=-1.0 / CHUNK
                     )
+                )
             if j == CHUNKS_PER_SEQ - 1:
                 early_statistics(group)
 
         def sum_squares(chunk, half):
             seq, j = divmod(chunk, CHUNKS_PER_SEQ)
             group = (seq, half)
+            if j == 0:
+                do_chores()
             squares = stage.tile([P, CHUNK], BF16, name="squares")
             nc.scalar.activation(
                 out=squares[:], in_=y[group][:, CHUNK * j : CHUNK * (j + 1)], func=ACT.Square,
-                bias=pivot[group][:, 1:2], scale=ROOT_SCALE, accum_out=sums[group][:, 1, j : j + 1],
+                bias=neg_pivot[group][:, 0:1], accum_out=sums[group][:, 1, j : j + 1],
             )
+            do_chore()
             if j == CHUNKS_PER_SEQ - 1:
                 late_statistics(group)
 
-        def add_columns(total, row, count):
-            nc.gpsimd.tensor_tensor(out=total, in0=row[:, 0:1], in1=row[:, 1:2], op=ALU.add)
-            for col in range(2, count):
-                nc.gpsimd.tensor_tensor(out=total, in0=total, in1=row[:, col : col + 1], op=ALU.add)
-
         def early_statistics(group):
-            total = per_group.tile([P, 1], F32, name="total")
-            add_columns(total[:], sums[group][:, 0, :], CHUNKS_PER_SEQ)
             neg_mean[group] = per_group.tile([P, 1], F32, name="neg_mean")
-            nc.gpsimd.tensor_scalar(
-                out=neg_mean[group][:], in0=total[:],
-                scalar1=-1.0 / FRAMES, scalar2=0.0, op0=ALU.mult, op1=ALU.add,
+            off_sq[group] = per_group.tile([P, 1], F32, name="off_sq")
+            terms = per_group.tile([P, CHUNKS_PER_SEQ], F32, name="terms")
+            chores.append(
+                lambda: nc.scalar.activation(
+                    out=terms[:], in_=sums[group][:, 0, 0:CHUNKS_PER_SEQ], func=ACT.Identity,
+                    scale=-1.0 / FRAMES, accum_out=neg_mean[group][:],
+                )
             )
-            off = per_group.tile([P, 1], F32, name="off")
-            nc.gpsimd.tensor_tensor(
-                out=off[:], in0=neg_mean[group][:], in1=pivot[group][:, 0:1], op=ALU.subtract
+            chores.append(
+                lambda: nc.scalar.activation(
+                    out=off_sq[group][:], in_=neg_mean[group][:], func=ACT.Square,
+                    bias=neg_pivot[group][:], scale=-1.0,
+                )
             )
-            off_sq = per_group.tile([P, 1], F32, name="off_sq")
-            nc.gpsimd.tensor_tensor(out=off_sq[:], in0=off[:], in1=off[:], op=ALU.mult)
-            rest = per_group.tile([P, 1], F32, name="rest")
-            nc.gpsimd.tensor_scalar(
-                out=rest[:], in0=off_sq[:], scalar1=-1.0, scalar2=EPS, op0=ALU.mult, op1=ALU.add
-            )
-            first_squares = per_group.tile([P, 1], F32, name="first_squares")
-            add_columns(first_squares[:], sums[group][:, 1, :], CHUNKS_PER_SEQ - 1)
-            base[group] = per_group.tile([P, 1], F32, name="base")
-            nc.gpsimd.tensor_tensor(out=base[group][:], in0=first_squares[:], in1=rest[:], op=ALU.add)
 
         def late_statistics(group):
-            var_eps = per_group.tile([P, 1], F32, name="var_eps")
-            nc.gpsimd.tensor_tensor(
-                out=var_eps[:], in0=base[group][:],
-                in1=sums[group][:, 1, CHUNKS_PER_SEQ - 1 : CHUNKS_PER_SEQ], op=ALU.add,
-            )
+            square_eps = per_group.tile([P, 1], F32, name="square_eps")
+            terms = per_group.tile([P, CHUNKS_PER_SEQ], F32, name="terms")
             rstd[group] = per_group.tile([P, 1], F32, name="rstd")
-            nc.gpsimd.tensor_tensor(out=rstd[group][:], in0=var_eps[:], in1=minus_half[:], op=ALU.pow)
             shift[group] = per_group.tile([P, 1], F32, name="shift")
-            nc.gpsimd.tensor_tensor(
-                out=shift[group][:], in0=neg_mean[group][:], in1=rstd[group][:], op=ALU.mult
+            chores.append(
+                lambda: nc.scalar.activation(
+                    out=terms[:], in_=sums[group][:, 1, 0:CHUNKS_PER_SEQ], func=ACT.Identity,
+                    bias=EPS / CHUNKS_PER_SEQ, scale=1.0 / FRAMES, accum_out=square_eps[:],
+                )
+            )
+            chores.append(
+                lambda: nc.scalar.activation(
+                    out=rstd[group][:], in_=off_sq[group][:], func=ACT.Abs_reciprocal_sqrt,
+                    bias=square_eps[:], scale=-1.0,
+                )
+            )
+            chores.append(
+                lambda: nc.scalar.activation(
+                    out=shift[group][:], in_=neg_mean[group][:], func=ACT.Identity, scale=rstd[group][:]
+                )
             )
 
         def normalise_and_store(seq, half, part, vector_cols):
             group = (seq, half)
+            if part == 0:
+                do_chores()
             first, last = NORM_PART * part, NORM_PART * (part + 1)
             split = first + vector_cols
             nc.vector.tensor_scalar(
                 out=y[group][:, first:split], in0=y[group][:, first:split],
-                scalar1=rstd[group][:, 0:1], scalar2=shift[group][:, 0:1], op0=ALU.mult, op1=ALU.add,
+                scalar1=neg_mean[group][:, 0:1], scalar2=rstd[group][:, 0:1], op0=ALU.add, op1=ALU.mult,
             )
             nc.scalar.activation(
                 out=y[group][:, split:last], in_=y[group][:, split:last], func=ACT.Identity,

@@ -292,6 +292,9 @@ def tile_transformerencoderblock_pa_t_kernel(tc, h_attn, x, masks, Wo, bo, out):
             return 0 <= chunk < CHUNKS
 
         for r in range(-LOAD_AHEAD, CHUNKS + LAG + NORM_BEHIND - CHUNKS_PER_SEQ + FRAMES // NORM_PART):
+            for half in range(HALVES):
+                if live(r - LAG * half - SQUARES_BEHIND):
+                    sum_squares(r - LAG * half - SQUARES_BEHIND, half)
             if live(r + FLIP_AHEAD):
                 flip_chunk(r + FLIP_AHEAD, r < 0)
             if r == -SPREAD_AHEAD:
@@ -307,13 +310,10 @@ def tile_transformerencoderblock_pa_t_kernel(tc, h_attn, x, masks, Wo, bo, out):
                 if live(r - LAG * half + MULTIPLY_AHEAD):
                     multiply(r - LAG * half + MULTIPLY_AHEAD, half)
             for half in range(HALVES):
-                if live(r - LAG * half - SQUARES_BEHIND):
-                    sum_squares(r - LAG * half - SQUARES_BEHIND, half)
-            for half in range(HALVES):
-                if live(r + FLIP_AHEAD):
-                    quantise_block(r + FLIP_AHEAD, half)
                 if live(r - LAG * half):
                     add_residual(r - LAG * half, half)
+                if live(r + FLIP_AHEAD):
+                    quantise_block(r + FLIP_AHEAD, half)
             for half in range(HALVES):
                 seq, part = divmod(r - LAG * half - NORM_BEHIND, CHUNKS_PER_SEQ)
                 if 0 <= seq < SEQS and part < FRAMES // NORM_PART:

@@ -34,6 +34,7 @@ SQUARES_BEHIND = 1
 NORM_BEHIND = CHUNKS_PER_SEQ + 1
 RESIDUAL_AHEAD = 5
 
+NORM_GPSIMD_COLS = 3 * NORM_PART // 4
 NORM_VECTOR_COLS = NORM_PART // 2
 NORM_VECTOR_COLS_END = 21 * NORM_PART // 32
 
@@ -58,15 +59,18 @@ def tile_transformerencoderblock_pa_t_kernel(tc, h_attn, x, masks, Wo, bo, out):
         raw, grouped = {}, {}
         codes, scales, mask_rows = {}, {}, {}
         product = {}
-        residual, y, sums, neg_pivot, neg_mean, off_sq, rstd, shift = {}, {}, {}, {}, {}, {}, {}, {}
+        residual, y, sums, neg_pivot, neg_mean, off_sq, affine, go = {}, {}, {}, {}, {}, {}, {}, {}
         chores = []
+
+        def add_chore(group, chore):
+            chores.append((group, chore))
 
         def do_chore():
             if chores:
-                chores.pop(0)()
+                chores.pop(0)[1]()
 
-        def do_chores():
-            while chores:
+        def finish_chores(group):
+            while any(waiting[0] == group for waiting in chores):
                 do_chore()
 
         def flip_two(rows_words, grouped_words, by_vector):
@@ -208,7 +212,8 @@ def tile_transformerencoderblock_pa_t_kernel(tc, h_attn, x, masks, Wo, bo, out):
             )
             if j == 0:
                 neg_pivot[group] = per_group.tile([P, 1], F32, name="neg_pivot")
-                chores.append(
+                add_chore(
+                    group,
                     lambda: nc.scalar.activation(
                         out=neg_pivot[group][:], in_=sums[group][:, 0, 0:1], func=ACT.Identity, scale=-1.0 / CHUNK
                     )
@@ -220,7 +225,7 @@ def tile_transformerencoderblock_pa_t_kernel(tc, h_attn, x, masks, Wo, bo, out):
             seq, j = divmod(chunk, CHUNKS_PER_SEQ)
             group = (seq, half)
             if j == 0:
-                do_chores()
+                finish_chores(group)
             squares = stage.tile([P, CHUNK], BF16, name="squares")
             nc.scalar.activation(
                 out=squares[:], in_=y[group][:, CHUNK * j : CHUNK * (j + 1)], func=ACT.Square,
@@ -234,13 +239,15 @@ def tile_transformerencoderblock_pa_t_kernel(tc, h_attn, x, masks, Wo, bo, out):
             neg_mean[group] = per_group.tile([P, 1], F32, name="neg_mean")
             off_sq[group] = per_group.tile([P, 1], F32, name="off_sq")
             terms = per_group.tile([P, CHUNKS_PER_SEQ], F32, name="terms")
-            chores.append(
+            add_chore(
+                group,
                 lambda: nc.scalar.activation(
                     out=terms[:], in_=sums[group][:, 0, 0:CHUNKS_PER_SEQ], func=ACT.Identity,
                     scale=-1.0 / FRAMES, accum_out=neg_mean[group][:],
                 )
             )
-            chores.append(
+            add_chore(
+                group,
                 lambda: nc.scalar.activation(
                     out=off_sq[group][:], in_=neg_mean[group][:], func=ACT.Square,
                     bias=neg_pivot[group][:], scale=-1.0,
@@ -250,39 +257,52 @@ def tile_transformerencoderblock_pa_t_kernel(tc, h_attn, x, masks, Wo, bo, out):
         def late_statistics(group):
             square_eps = per_group.tile([P, 1], F32, name="square_eps")
             terms = per_group.tile([P, CHUNKS_PER_SEQ], F32, name="terms")
-            rstd[group] = per_group.tile([P, 1], F32, name="rstd")
-            shift[group] = per_group.tile([P, 1], F32, name="shift")
-            chores.append(
+            affine[group] = per_group.tile([P, 2], F32, name="affine")
+            add_chore(
+                group,
                 lambda: nc.scalar.activation(
                     out=terms[:], in_=sums[group][:, 1, 0:CHUNKS_PER_SEQ], func=ACT.Identity,
                     bias=EPS / CHUNKS_PER_SEQ, scale=1.0 / FRAMES, accum_out=square_eps[:],
                 )
             )
-            chores.append(
+            add_chore(
+                group,
                 lambda: nc.scalar.activation(
-                    out=rstd[group][:], in_=off_sq[group][:], func=ACT.Abs_reciprocal_sqrt,
+                    out=affine[group][:, 0:1], in_=off_sq[group][:], func=ACT.Abs_reciprocal_sqrt,
                     bias=square_eps[:], scale=-1.0,
                 )
             )
-            chores.append(
+            add_chore(
+                group,
                 lambda: nc.scalar.activation(
-                    out=shift[group][:], in_=neg_mean[group][:], func=ACT.Identity, scale=rstd[group][:]
+                    out=affine[group][:, 1:2], in_=neg_mean[group][:], func=ACT.Identity, scale=affine[group][:, 0:1]
                 )
             )
 
-        def normalise_and_store(seq, half, part, vector_cols):
+        def send_gpsimd(group):
+            finish_chores(group)
+            go[group] = per_group.tile([P, 2], F32, name="go")
+            nc.vector.tensor_copy(out=go[group][:], in_=affine[group][:])
+
+        def normalise_and_store(seq, half, part, vector_cols, gpsimd_cols):
             group = (seq, half)
-            if part == 0:
-                do_chores()
+            finish_chores(group)
             first, last = NORM_PART * part, NORM_PART * (part + 1)
-            split = first + vector_cols
-            nc.vector.tensor_scalar(
-                out=y[group][:, first:split], in0=y[group][:, first:split],
-                scalar1=neg_mean[group][:, 0:1], scalar2=rstd[group][:, 0:1], op0=ALU.add, op1=ALU.mult,
-            )
+            to_vector = first + gpsimd_cols
+            to_scalar = to_vector + vector_cols
+            if gpsimd_cols:
+                nc.gpsimd.tensor_scalar(
+                    out=y[group][:, first:to_vector], in0=y[group][:, first:to_vector],
+                    scalar1=go[group][:, 0:1], scalar2=go[group][:, 1:2], op0=ALU.mult, op1=ALU.add,
+                )
+            if vector_cols:
+                nc.vector.tensor_scalar(
+                    out=y[group][:, to_vector:to_scalar], in0=y[group][:, to_vector:to_scalar],
+                    scalar1=neg_mean[group][:, 0:1], scalar2=affine[group][:, 0:1], op0=ALU.add, op1=ALU.mult,
+                )
             nc.scalar.activation(
-                out=y[group][:, split:last], in_=y[group][:, split:last], func=ACT.Identity,
-                bias=shift[group][:, 0:1], scale=rstd[group][:, 0:1],
+                out=y[group][:, to_scalar:last], in_=y[group][:, to_scalar:last], func=ACT.Identity,
+                bias=affine[group][:, 1:2], scale=affine[group][:, 0:1],
             )
             nc.sync.dma_start(
                 out=out_halves[seq, half, :, first:last], in_=y[group][:, first:last]
@@ -317,8 +337,16 @@ def tile_transformerencoderblock_pa_t_kernel(tc, h_attn, x, masks, Wo, bo, out):
             for half in range(HALVES):
                 seq, part = divmod(r - LAG * half - NORM_BEHIND, CHUNKS_PER_SEQ)
                 if 0 <= seq < SEQS and part < FRAMES // NORM_PART:
-                    busy = r < CHUNKS + LAG
-                    normalise_and_store(seq, half, part, NORM_VECTOR_COLS if busy else NORM_VECTOR_COLS_END)
+                    if r < CHUNKS:
+                        normalise_and_store(seq, half, part, 0, NORM_GPSIMD_COLS)
+                    elif r < CHUNKS + LAG:
+                        normalise_and_store(seq, half, part, NORM_VECTOR_COLS, 0)
+                    else:
+                        normalise_and_store(seq, half, part, NORM_VECTOR_COLS_END, 0)
+            for half in range(HALVES):
+                seq, part = divmod(r + 1 - LAG * half - NORM_BEHIND, CHUNKS_PER_SEQ)
+                if 0 <= seq < SEQS and part < FRAMES // NORM_PART and r + 1 < CHUNKS:
+                    send_gpsimd((seq, half))
             for half in range(HALVES):
                 seq, j = divmod(r - LAG * half + RESIDUAL_AHEAD, CHUNKS_PER_SEQ)
                 if 0 <= seq < SEQS and j == 0:

@@ -26,24 +26,25 @@ HALVES = C_OUT // P
 NORM_PART = 2 * CHUNK
 
 LAG = 2
-LOAD_AHEAD = 6
+LOAD_AHEAD = 4
 FLIP_AHEAD = 2
 SPREAD_AHEAD = 1
 MULTIPLY_AHEAD = 1
 SQUARES_BEHIND = 1
 NORM_BEHIND = CHUNKS_PER_SEQ + 1
-RESIDUAL_AHEAD = 5
+RESIDUAL_AHEAD = 2
 
+QUARTER = FRAMES // 4
 NORM_GPSIMD_COLS = 3 * NORM_PART // 4
-NORM_VECTOR_COLS = NORM_PART // 2
-NORM_VECTOR_COLS_END = 21 * NORM_PART // 32
+HALF_WINDOW_COLS = NORM_GPSIMD_COLS // 2
 
 
 def tile_transformerencoderblock_pa_t_kernel(tc, h_attn, x, masks, Wo, bo, out):
     nc = tc.nc
     with ExitStack() as ctx:
         const = ctx.enter_context(tc.tile_pool(name="const", bufs=1))
-        blocks_in = ctx.enter_context(tc.tile_pool(name="blocks_in", bufs=2 * (LOAD_AHEAD - FLIP_AHEAD)))
+        blocks_in = ctx.enter_context(tc.tile_pool(name="blocks_in", bufs=2 * LOAD_AHEAD))
+        steps_in = ctx.enter_context(tc.tile_pool(name="steps_in", bufs=HALVES * (RESIDUAL_AHEAD + 1)))
         stage = ctx.enter_context(tc.tile_pool(name="stage", bufs=4))
         per_chunk = ctx.enter_context(tc.tile_pool(name="per_chunk", bufs=FLIP_AHEAD + LAG))
         per_group = ctx.enter_context(tc.tile_pool(name="per_group", bufs=4))
@@ -54,7 +55,6 @@ def tile_transformerencoderblock_pa_t_kernel(tc, h_attn, x, masks, Wo, bo, out):
         make_identity(nc, ident_f32[:])
         one = const.tile([P, 2], F32)
         nc.vector.memset(one[:], 1.0)
-        nc.scalar.activation(out=one[:, 1:2], in_=one[:, 0:1], func=ACT.Abs_reciprocal_sqrt)
 
         raw, grouped = {}, {}
         codes, scales, mask_rows = {}, {}, {}
@@ -97,7 +97,10 @@ def tile_transformerencoderblock_pa_t_kernel(tc, h_attn, x, masks, Wo, bo, out):
             out=small_rows[mask_row_count : mask_row_count + 1, :], in_=bo.rearrange("(o c) -> o c", o=1)
         )
         w_raw = const.tile([P, HALVES * C_IN], BF16)
-        nc.scalar.dma_start(out=w_raw[:], in_=Wo.rearrange("(p h) k -> p (h k)", h=HALVES))
+        def load_weights():
+            nc.sync.dma_start(out=w_raw[:], in_=Wo.rearrange("(p h) k -> p (h k)", h=HALVES))
+
+        nc.scalar.activation(out=one[:, 1:2], in_=one[:, 0:1], func=ACT.Abs_reciprocal_sqrt)
         mask_words = const.tile([P, mask_row_count], F32)
         bias_cols = const.tile([P, HALVES], F32)
         w_grouped = const.tile([P, HALVES * C_IN], BF16, align_bytes=64)
@@ -111,35 +114,38 @@ def tile_transformerencoderblock_pa_t_kernel(tc, h_attn, x, masks, Wo, bo, out):
             nc.vector.tensor_copy(
                 out=bias_cols[:], in_=small_cols[:, mask_row_count : mask_row_count + 1].bitcast(BF16)
             )
+        def flip_weights():
             flip_two(w_raw[:].bitcast(F32), w_grouped[:].bitcast(F32), True)
+
+        def quantise_weights():
             nc.vector.quantize_mx(out=w_codes[:].bitcast(FP8X4), scales=w_scales[:], in_=w_grouped[:])
 
         x_halves = x.rearrange("n (p h) t -> n h p t", h=HALVES)
         out_halves = out.rearrange("n (p h) t -> n h p t", h=HALVES)
 
-        def load_chunk(chunk):
+        def load_block(chunk, i, pieces=1):
             seq, j = divmod(chunk, CHUNKS_PER_SEQ)
-            for i in range(CHUNK // BLOCK):
-                first = CHUNK * j + BLOCK * i
-                raw[(chunk, i)] = blocks_in.tile([P, ROWS * C_IN], BF16, name="raw")
-                nc.sync.dma_start(
-                    out=raw[(chunk, i)][:],
-                    in_=h_attn[seq, first : first + BLOCK, :].rearrange("(p a) k -> p (a k)", a=ROWS),
-                )
+            first = CHUNK * j + BLOCK * i
+            raw[(chunk, i)] = blocks_in.tile([P, ROWS * C_IN], BF16, name="raw")
+            rows = h_attn[seq, first : first + BLOCK, :].rearrange("(p a) k -> p (a k)", a=ROWS)
+            width = ROWS * C_IN // pieces
+            for piece in range(pieces):
+                cols = slice(width * piece, width * (piece + 1))
+                nc.sync.dma_start(out=raw[(chunk, i)][:, cols], in_=rows[:, cols])
 
-        def load_residual(seq, half):
-            group = (seq, half)
-            residual[group] = per_group.tile([P, FRAMES], BF16, name="residual")
-            nc.sync.dma_start(out=residual[group][:], in_=x_halves[seq, half])
+        def load_residual(chunk, half):
+            seq, j = divmod(chunk, CHUNKS_PER_SEQ)
+            cols = slice(CHUNK * j, CHUNK * (j + 1))
+            residual[(chunk, half)] = steps_in.tile([P, CHUNK], BF16, name="residual")
+            nc.sync.dma_start(out=residual[(chunk, half)][:], in_=x_halves[seq, half, :, cols])
 
-        def flip_chunk(chunk, vector_helps):
-            for i in range(CHUNK // BLOCK):
-                grouped[(chunk, i)] = stage.tile([P, 4 * BLOCK], BF16, name="grouped", align_bytes=64)
-                raw_words = raw[(chunk, i)][:].bitcast(F32)
-                grouped_words = grouped[(chunk, i)][:].bitcast(F32)
-                for pair in range(ROWS // 2):
-                    cols = slice(2 * WORDS * pair, 2 * WORDS * (pair + 1))
-                    flip_two(raw_words[:, cols], grouped_words[:, cols], vector_helps and pair == 1)
+        def flip_block(chunk, i, by_vector=()):
+            grouped[(chunk, i)] = stage.tile([P, 4 * BLOCK], BF16, name="grouped", align_bytes=64)
+            raw_words = raw[(chunk, i)][:].bitcast(F32)
+            grouped_words = grouped[(chunk, i)][:].bitcast(F32)
+            for pair in range(ROWS // 2):
+                cols = slice(2 * WORDS * pair, 2 * WORDS * (pair + 1))
+                flip_two(raw_words[:, cols], grouped_words[:, cols], pair in by_vector)
 
         def spread_mask(chunk):
             mask_rows[chunk] = per_chunk.tile([P, CHUNK], BF16, name="mask_rows")
@@ -197,18 +203,25 @@ def tile_transformerencoderblock_pa_t_kernel(tc, h_attn, x, masks, Wo, bo, out):
                     op1=ALU.mult,
                 )
 
-        def add_residual(chunk, half):
+        def add_residual(chunk, half, pieces=1):
             seq, j = divmod(chunk, CHUNKS_PER_SEQ)
-            group = (seq, half)
-            cols = slice(CHUNK * j, CHUNK * (j + 1))
+            for piece in range(pieces):
+                add_residual_piece(
+                    (seq, half), j, residual[(chunk, half)], CHUNK // pieces * piece, CHUNK // pieces, j + piece
+                )
+            if j == CHUNKS_PER_SEQ - 1:
+                early_statistics((seq, half), CHUNKS_PER_SEQ - 1 + pieces)
+
+        def add_residual_piece(group, j, x_step, first, width, sum_col):
+            cols = slice(CHUNK * j + first, CHUNK * j + first + width)
             nc.vector.scalar_tensor_tensor(
                 out=y[group][:, cols],
                 in0=y[group][:, cols],
                 scalar=1.0,
-                in1=residual[group][:, cols],
+                in1=x_step[:, first : first + width],
                 op0=ALU.mult,
                 op1=ALU.add,
-                accum_out=sums[group][:, 0, j : j + 1],
+                accum_out=sums[group][:, 0, sum_col : sum_col + 1],
             )
             if j == 0:
                 neg_pivot[group] = per_group.tile([P, 1], F32, name="neg_pivot")
@@ -218,31 +231,31 @@ def tile_transformerencoderblock_pa_t_kernel(tc, h_attn, x, masks, Wo, bo, out):
                         out=neg_pivot[group][:], in_=sums[group][:, 0, 0:1], func=ACT.Identity, scale=-1.0 / CHUNK
                     )
                 )
-            if j == CHUNKS_PER_SEQ - 1:
-                early_statistics(group)
-
-        def sum_squares(chunk, half):
+        def sum_squares(chunk, half, pieces=1):
             seq, j = divmod(chunk, CHUNKS_PER_SEQ)
             group = (seq, half)
             if j == 0:
                 finish_chores(group)
-            squares = stage.tile([P, CHUNK], BF16, name="squares")
-            nc.scalar.activation(
-                out=squares[:], in_=y[group][:, CHUNK * j : CHUNK * (j + 1)], func=ACT.Square,
-                bias=neg_pivot[group][:, 0:1], accum_out=sums[group][:, 1, j : j + 1],
-            )
-            do_chore()
+            width = CHUNK // pieces
+            for piece in range(pieces):
+                first = CHUNK * j + width * piece
+                squares = stage.tile([P, CHUNK], BF16, name="squares")
+                nc.scalar.activation(
+                    out=squares[:, 0:width], in_=y[group][:, first : first + width], func=ACT.Square,
+                    bias=neg_pivot[group][:, 0:1], accum_out=sums[group][:, 1, j + piece : j + piece + 1],
+                )
+                do_chore()
             if j == CHUNKS_PER_SEQ - 1:
-                late_statistics(group)
+                late_statistics(group, CHUNKS_PER_SEQ - 1 + pieces)
 
-        def early_statistics(group):
+        def early_statistics(group, count):
             neg_mean[group] = per_group.tile([P, 1], F32, name="neg_mean")
             off_sq[group] = per_group.tile([P, 1], F32, name="off_sq")
-            terms = per_group.tile([P, CHUNKS_PER_SEQ], F32, name="terms")
+            terms = per_group.tile([P, 8], F32, name="terms")
             add_chore(
                 group,
                 lambda: nc.scalar.activation(
-                    out=terms[:], in_=sums[group][:, 0, 0:CHUNKS_PER_SEQ], func=ACT.Identity,
+                    out=terms[:, 0:count], in_=sums[group][:, 0, 0:count], func=ACT.Identity,
                     scale=-1.0 / FRAMES, accum_out=neg_mean[group][:],
                 )
             )
@@ -254,15 +267,15 @@ def tile_transformerencoderblock_pa_t_kernel(tc, h_attn, x, masks, Wo, bo, out):
                 )
             )
 
-        def late_statistics(group):
+        def late_statistics(group, count):
             square_eps = per_group.tile([P, 1], F32, name="square_eps")
-            terms = per_group.tile([P, CHUNKS_PER_SEQ], F32, name="terms")
+            terms = per_group.tile([P, 8], F32, name="terms")
             affine[group] = per_group.tile([P, 2], F32, name="affine")
             add_chore(
                 group,
                 lambda: nc.scalar.activation(
-                    out=terms[:], in_=sums[group][:, 1, 0:CHUNKS_PER_SEQ], func=ACT.Identity,
-                    bias=EPS / CHUNKS_PER_SEQ, scale=1.0 / FRAMES, accum_out=square_eps[:],
+                    out=terms[:, 0:count], in_=sums[group][:, 1, 0:count], func=ACT.Identity,
+                    bias=EPS / count, scale=1.0 / FRAMES, accum_out=square_eps[:],
                 )
             )
             add_chore(
@@ -284,70 +297,130 @@ def tile_transformerencoderblock_pa_t_kernel(tc, h_attn, x, masks, Wo, bo, out):
             go[group] = per_group.tile([P, 2], F32, name="go")
             nc.vector.tensor_copy(out=go[group][:], in_=affine[group][:])
 
-        def normalise_and_store(seq, half, part, vector_cols, gpsimd_cols):
-            group = (seq, half)
+        def normalise(group, first, last, engine):
             finish_chores(group)
-            first, last = NORM_PART * part, NORM_PART * (part + 1)
-            to_vector = first + gpsimd_cols
-            to_scalar = to_vector + vector_cols
-            if gpsimd_cols:
+            cols = y[group][:, first:last]
+            if engine == "gpsimd":
                 nc.gpsimd.tensor_scalar(
-                    out=y[group][:, first:to_vector], in0=y[group][:, first:to_vector],
-                    scalar1=go[group][:, 0:1], scalar2=go[group][:, 1:2], op0=ALU.mult, op1=ALU.add,
+                    out=cols, in0=cols, scalar1=go[group][:, 0:1], scalar2=go[group][:, 1:2], op0=ALU.mult, op1=ALU.add
                 )
-            if vector_cols:
+            elif engine == "vector":
                 nc.vector.tensor_scalar(
-                    out=y[group][:, to_vector:to_scalar], in0=y[group][:, to_vector:to_scalar],
-                    scalar1=neg_mean[group][:, 0:1], scalar2=affine[group][:, 0:1], op0=ALU.add, op1=ALU.mult,
+                    out=cols, in0=cols, scalar1=neg_mean[group][:, 0:1], scalar2=affine[group][:, 0:1],
+                    op0=ALU.add, op1=ALU.mult,
                 )
-            nc.scalar.activation(
-                out=y[group][:, to_scalar:last], in_=y[group][:, to_scalar:last], func=ACT.Identity,
-                bias=affine[group][:, 1:2], scale=affine[group][:, 0:1],
-            )
-            nc.sync.dma_start(
-                out=out_halves[seq, half, :, first:last], in_=y[group][:, first:last]
-            )
+            else:
+                nc.scalar.activation(
+                    out=cols, in_=cols, func=ACT.Identity, bias=affine[group][:, 1:2], scale=affine[group][:, 0:1]
+                )
+
+        def parts_of_round(r):
+            for half in range(HALVES):
+                seq, part = divmod(r - LAG * half - NORM_BEHIND, CHUNKS_PER_SEQ)
+                if 0 <= seq < SEQS and part < FRAMES // NORM_PART:
+                    return [((seq, half), part)]
+            return []
+
+        def store(group, first, last):
+            seq, half = group
+            nc.sync.dma_start(out=out_halves[seq, half, :, first:last], in_=y[group][:, first:last])
 
         def live(chunk):
             return 0 <= chunk < CHUNKS
 
-        for r in range(-LOAD_AHEAD, CHUNKS + LAG + NORM_BEHIND - CHUNKS_PER_SEQ + FRAMES // NORM_PART):
+        load_block(0, 0, 2)
+        load_weights()
+        load_block(0, 1)
+        load_residual(0, 0)
+        for i in range(CHUNK // BLOCK):
+            load_block(1, i)
+        for i in range(CHUNK // BLOCK):
+            load_block(2, i)
+        load_residual(1, 0)
+        for i in range(CHUNK // BLOCK):
+            load_block(3, i)
+        flip_block(0, 0)
+        prepare_small_inputs()
+        flip_weights()
+        flip_block(0, 1)
+        quantise_block(0, 0)
+        quantise_weights()
+        quantise_block(0, 1)
+        spread_mask(0)
+        flip_block(1, 0)
+        multiply(0, 0)
+        flip_block(1, 1)
+
+        squared_late = [(CHUNKS - 1, 0), (CHUNKS - LAG - 1, 1), (CHUNKS - LAG, 1), (CHUNKS - 1, 1)]
+        for r in range(CHUNKS + LAG):
             for half in range(HALVES):
-                if live(r - LAG * half - SQUARES_BEHIND):
-                    sum_squares(r - LAG * half - SQUARES_BEHIND, half)
-            if live(r + FLIP_AHEAD):
-                flip_chunk(r + FLIP_AHEAD, r < 0)
-            if r == -SPREAD_AHEAD:
-                prepare_small_inputs()
+                chunk = r - LAG * half - SQUARES_BEHIND
+                if live(chunk) and (chunk, half) not in squared_late:
+                    sum_squares(chunk, half)
+            for i in range(CHUNK // BLOCK):
+                if live(r + FLIP_AHEAD):
+                    flip_block(r + FLIP_AHEAD, i)
             if live(r + SPREAD_AHEAD):
                 spread_mask(r + SPREAD_AHEAD)
-            if live(r + LOAD_AHEAD):
-                load_chunk(r + LOAD_AHEAD)
+            for i in range(CHUNK // BLOCK):
+                if live(r + LOAD_AHEAD):
+                    load_block(r + LOAD_AHEAD, i)
+            for half in range(HALVES):
+                if live(r - LAG * half + RESIDUAL_AHEAD):
+                    load_residual(r - LAG * half + RESIDUAL_AHEAD, half)
             for half in range(HALVES):
                 if live(r - LAG * half):
                     add_bias_and_mask(r - LAG * half, half)
+            if r == 0:
+                quantise_block(1, 0)
+                quantise_block(1, 1)
             for half in range(HALVES):
                 if live(r - LAG * half + MULTIPLY_AHEAD):
                     multiply(r - LAG * half + MULTIPLY_AHEAD, half)
+            if r == CHUNKS:
+                normalise((2, 0), 0, QUARTER, "vector")
+                store((2, 0), 0, QUARTER)
             for half in range(HALVES):
                 if live(r - LAG * half):
-                    add_residual(r - LAG * half, half)
+                    add_residual(r - LAG * half, half, 2 if r == CHUNKS + LAG - 1 else 1)
                 if live(r + FLIP_AHEAD):
                     quantise_block(r + FLIP_AHEAD, half)
-            for half in range(HALVES):
-                seq, part = divmod(r - LAG * half - NORM_BEHIND, CHUNKS_PER_SEQ)
-                if 0 <= seq < SEQS and part < FRAMES // NORM_PART:
-                    if r < CHUNKS:
-                        normalise_and_store(seq, half, part, 0, NORM_GPSIMD_COLS)
-                    elif r < CHUNKS + LAG:
-                        normalise_and_store(seq, half, part, NORM_VECTOR_COLS, 0)
-                    else:
-                        normalise_and_store(seq, half, part, NORM_VECTOR_COLS_END, 0)
-            for half in range(HALVES):
-                seq, part = divmod(r + 1 - LAG * half - NORM_BEHIND, CHUNKS_PER_SEQ)
-                if 0 <= seq < SEQS and part < FRAMES // NORM_PART and r + 1 < CHUNKS:
-                    send_gpsimd((seq, half))
-            for half in range(HALVES):
-                seq, j = divmod(r - LAG * half + RESIDUAL_AHEAD, CHUNKS_PER_SEQ)
-                if 0 <= seq < SEQS and j == 0:
-                    load_residual(seq, half)
+            if r < CHUNKS:
+                for group, part in parts_of_round(r):
+                    first, last = NORM_PART * part, NORM_PART * (part + 1)
+                    if group == (1, 1):
+                        first, last = QUARTER, 3 * QUARTER
+                    normalise(group, first, first + NORM_GPSIMD_COLS, "gpsimd")
+                    normalise(group, first + NORM_GPSIMD_COLS, last, "scalar")
+                    store(group, first, last)
+            if r + 1 < CHUNKS:
+                for group, part in parts_of_round(r + 1):
+                    send_gpsimd(group)
+
+            if r == CHUNKS - 2:
+                normalise((1, 1), 0, QUARTER, "scalar")
+                store((1, 1), 0, QUARTER)
+            if r == CHUNKS - 1:
+                do_chore()
+                sum_squares(CHUNKS - 1, 0)
+                finish_chores((2, 0))
+                send_gpsimd((1, 1))
+            if r == CHUNKS:
+                normalise((1, 1), 3 * QUARTER, 3 * QUARTER + HALF_WINDOW_COLS, "gpsimd")
+                normalise((1, 1), 3 * QUARTER + HALF_WINDOW_COLS, FRAMES, "scalar")
+                store((1, 1), 3 * QUARTER, FRAMES)
+                normalise((2, 0), QUARTER, 2 * QUARTER, "scalar")
+                store((2, 0), QUARTER, 2 * QUARTER)
+                sum_squares(CHUNKS - LAG - 1, 1)
+                sum_squares(CHUNKS - LAG, 1)
+                send_gpsimd((2, 0))
+            if r == CHUNKS + 1:
+                normalise((2, 0), 3 * QUARTER, 3 * QUARTER + HALF_WINDOW_COLS, "gpsimd")
+                normalise((2, 0), 3 * QUARTER + HALF_WINDOW_COLS, FRAMES, "scalar")
+                store((2, 0), 3 * QUARTER, FRAMES)
+                sum_squares(CHUNKS - 1, 1, 2)
+                normalise((2, 0), 2 * QUARTER, 3 * QUARTER, "vector")
+                store((2, 0), 2 * QUARTER, 3 * QUARTER)
+        for first, last in ((0, BLOCK), (BLOCK, QUARTER), (QUARTER, 2 * QUARTER), (2 * QUARTER, FRAMES)):
+            normalise((2, 1), first, last, "vector")
+            store((2, 1), first, last)

@@ -53,13 +53,14 @@ def tile_transformerencoderblock_pa_t_kernel(tc, h_attn, x, masks, Wo, bo, out):
 
         ident_f32 = const.tile([P, P], F32)
         make_identity(nc, ident_f32[:])
-        one = const.tile([P, 2], F32)
-        nc.vector.memset(one[:], 1.0)
+
+        last_code = const.tile([P, 1], U32)
+        last_sum = const.tile([P, 1], F32)
 
         raw, grouped = {}, {}
         codes, scales, mask_rows = {}, {}, {}
         product = {}
-        residual, y, sums, neg_pivot, neg_mean, off_sq, affine, go = {}, {}, {}, {}, {}, {}, {}, {}
+        residual, y, sums, neg_pivot, neg_mean, off_sq, affine = {}, {}, {}, {}, {}, {}, {}
         chores = []
 
         def add_chore(group, chore):
@@ -89,6 +90,8 @@ def tile_transformerencoderblock_pa_t_kernel(tc, h_attn, x, masks, Wo, bo, out):
 
         small_rows = const.tile([P, 2 * P], BF16)
         nc.vector.memset(small_rows[:], 0.0)
+        one = const.tile([P, 2], F32)
+        nc.vector.memset(one[:], 1.0)
         mask_row_count = SEQS * FRAMES // (2 * P)
         nc.scalar.dma_start(
             out=small_rows[0:mask_row_count, :], in_=masks.rearrange("n o (i r) -> (n o i) r", r=2 * P)
@@ -292,17 +295,15 @@ def tile_transformerencoderblock_pa_t_kernel(tc, h_attn, x, masks, Wo, bo, out):
                 )
             )
 
-        def send_gpsimd(group):
-            finish_chores(group)
-            go[group] = per_group.tile([P, 2], F32, name="go")
-            nc.vector.tensor_copy(out=go[group][:], in_=affine[group][:])
+        def hold_gpsimd(copy_of, written_last):
+            nc.gpsimd.tensor_copy(out=copy_of[:], in_=written_last)
 
         def normalise(group, first, last, engine):
             finish_chores(group)
             cols = y[group][:, first:last]
             if engine == "gpsimd":
                 nc.gpsimd.tensor_scalar(
-                    out=cols, in0=cols, scalar1=go[group][:, 0:1], scalar2=go[group][:, 1:2], op0=ALU.mult, op1=ALU.add
+                    out=cols, in0=cols, scalar1=affine[group][:, 0:1], scalar2=affine[group][:, 1:2], op0=ALU.mult, op1=ALU.add
                 )
             elif engine == "vector":
                 nc.vector.tensor_scalar(
@@ -330,18 +331,18 @@ def tile_transformerencoderblock_pa_t_kernel(tc, h_attn, x, masks, Wo, bo, out):
 
         load_block(0, 0, 2)
         load_weights()
-        load_block(0, 1)
-        load_residual(0, 0)
+        load_block(0, 1, 2)
         for i in range(CHUNK // BLOCK):
-            load_block(1, i)
+            load_block(1, i, 2)
+        load_residual(0, 0)
         for i in range(CHUNK // BLOCK):
             load_block(2, i)
         load_residual(1, 0)
         for i in range(CHUNK // BLOCK):
             load_block(3, i)
         flip_block(0, 0)
-        prepare_small_inputs()
         flip_weights()
+        prepare_small_inputs()
         flip_block(0, 1)
         quantise_block(0, 0)
         quantise_weights()
@@ -393,10 +394,6 @@ def tile_transformerencoderblock_pa_t_kernel(tc, h_attn, x, masks, Wo, bo, out):
                     normalise(group, first, first + NORM_GPSIMD_COLS, "gpsimd")
                     normalise(group, first + NORM_GPSIMD_COLS, last, "scalar")
                     store(group, first, last)
-            if r + 1 < CHUNKS:
-                for group, part in parts_of_round(r + 1):
-                    send_gpsimd(group)
-
             if r == CHUNKS - 2:
                 normalise((1, 1), 0, QUARTER, "scalar")
                 store((1, 1), 0, QUARTER)
@@ -404,7 +401,6 @@ def tile_transformerencoderblock_pa_t_kernel(tc, h_attn, x, masks, Wo, bo, out):
                 do_chore()
                 sum_squares(CHUNKS - 1, 0)
                 finish_chores((2, 0))
-                send_gpsimd((1, 1))
             if r == CHUNKS:
                 normalise((1, 1), 3 * QUARTER, 3 * QUARTER + HALF_WINDOW_COLS, "gpsimd")
                 normalise((1, 1), 3 * QUARTER + HALF_WINDOW_COLS, FRAMES, "scalar")
@@ -413,7 +409,6 @@ def tile_transformerencoderblock_pa_t_kernel(tc, h_attn, x, masks, Wo, bo, out):
                 store((2, 0), QUARTER, 2 * QUARTER)
                 sum_squares(CHUNKS - LAG - 1, 1)
                 sum_squares(CHUNKS - LAG, 1)
-                send_gpsimd((2, 0))
             if r == CHUNKS + 1:
                 normalise((2, 0), 3 * QUARTER, 3 * QUARTER + HALF_WINDOW_COLS, "gpsimd")
                 normalise((2, 0), 3 * QUARTER + HALF_WINDOW_COLS, FRAMES, "scalar")
@@ -421,6 +416,13 @@ def tile_transformerencoderblock_pa_t_kernel(tc, h_attn, x, masks, Wo, bo, out):
                 sum_squares(CHUNKS - 1, 1, 2)
                 normalise((2, 0), 2 * QUARTER, 3 * QUARTER, "vector")
                 store((2, 0), 2 * QUARTER, 3 * QUARTER)
+            if r >= NORM_BEHIND - 1:
+                if live(r + FLIP_AHEAD):
+                    hold_gpsimd(last_code, codes[r + FLIP_AHEAD][:, CHUNK - 1 : CHUNK])
+                elif live(r - LAG):
+                    seq, j = divmod(r - LAG, CHUNKS_PER_SEQ)
+                    hold_gpsimd(last_sum, sums[(seq, 1)][:, 0, j : j + 1])
+
         for first, last in ((0, BLOCK), (BLOCK, QUARTER), (QUARTER, 2 * QUARTER), (2 * QUARTER, FRAMES)):
             normalise((2, 1), first, last, "vector")
             store((2, 1), first, last)

@@ -29,6 +29,7 @@ LAG = 2
 LOAD_AHEAD = 4
 FLIP_AHEAD = 2
 SPREAD_AHEAD = 1
+MASK_AHEAD = 3
 MULTIPLY_AHEAD = 1
 SQUARES_BEHIND = 1
 NORM_BEHIND = CHUNKS_PER_SEQ + 1
@@ -45,6 +46,7 @@ def tile_transformerencoderblock_pa_t_kernel(tc, h_attn, x, masks, Wo, bo, out):
         const = ctx.enter_context(tc.tile_pool(name="const", bufs=1))
         blocks_in = ctx.enter_context(tc.tile_pool(name="blocks_in", bufs=2 * LOAD_AHEAD))
         steps_in = ctx.enter_context(tc.tile_pool(name="steps_in", bufs=HALVES * (RESIDUAL_AHEAD + 1)))
+        masks_in = ctx.enter_context(tc.tile_pool(name="masks_in", bufs=SEQS))
         stage = ctx.enter_context(tc.tile_pool(name="stage", bufs=4))
         per_chunk = ctx.enter_context(tc.tile_pool(name="per_chunk", bufs=FLIP_AHEAD + LAG))
         per_group = ctx.enter_context(tc.tile_pool(name="per_group", bufs=4))
@@ -150,8 +152,13 @@ def tile_transformerencoderblock_pa_t_kernel(tc, h_attn, x, masks, Wo, bo, out):
                 cols = slice(2 * WORDS * pair, 2 * WORDS * (pair + 1))
                 flip_two(raw_words[:, cols], grouped_words[:, cols], pair in by_vector)
 
+        def load_mask(seq):
+            mask_rows[seq] = masks_in.tile([P, FRAMES], BF16, name="mask_rows")
+            nc.sync.dma_start(out=mask_rows[seq][:], in_=masks[seq, 0, :].partition_broadcast(P))
+
         def spread_mask(chunk):
-            mask_rows[chunk] = per_chunk.tile([P, CHUNK], BF16, name="mask_rows")
+            if chunk == 0:
+                mask_rows[0] = masks_in.tile([P, FRAMES], BF16, name="mask_rows")
             spread = psum.tile([P, CHUNK // 2], F32, tag="spread", bufs=1)
             for i in range(CHUNK // (2 * P)):
                 col = CHUNK // (2 * P) * chunk + i
@@ -160,7 +167,9 @@ def tile_transformerencoderblock_pa_t_kernel(tc, h_attn, x, masks, Wo, bo, out):
                     mask_words[:, col : col + 1].to_broadcast([P, P]),
                     ident_f32[:],
                 )
-            nc.scalar.copy(out=mask_rows[chunk][:], in_=spread[:].bitcast(BF16))
+            nc.scalar.copy(
+                out=mask_rows[0][:, CHUNK * chunk : CHUNK * (chunk + 1)], in_=spread[:].bitcast(BF16)
+            )
             do_chore()
 
         def quantise_block(chunk, i):
@@ -195,13 +204,12 @@ def tile_transformerencoderblock_pa_t_kernel(tc, h_attn, x, masks, Wo, bo, out):
                 y[group] = per_group.tile([P, FRAMES], F32, name="y")
                 sums[group] = per_group.tile([P, 2, 8], F32, name="sums")
             for i in range(CHUNK // BLOCK):
-                cols = slice(BLOCK * i, BLOCK * (i + 1))
                 first = CHUNK * j + BLOCK * i
                 nc.vector.scalar_tensor_tensor(
                     out=y[group][:, first : first + BLOCK].rearrange("e (p a) -> e p a", a=ROWS),
                     in0=product[(chunk, half, i)][:].rearrange("e (a p) -> e p a", a=ROWS),
                     scalar=bias_cols[:, half : half + 1],
-                    in1=mask_rows[chunk][:, cols].rearrange("e (p a) -> e p a", a=ROWS),
+                    in1=mask_rows[seq][:, first : first + BLOCK].rearrange("e (p a) -> e p a", a=ROWS),
                     op0=ALU.add,
                     op1=ALU.mult,
                 )
@@ -361,7 +369,7 @@ def tile_transformerencoderblock_pa_t_kernel(tc, h_attn, x, masks, Wo, bo, out):
             for i in range(CHUNK // BLOCK):
                 if live(r + FLIP_AHEAD):
                     flip_block(r + FLIP_AHEAD, i)
-            if live(r + SPREAD_AHEAD):
+            if r + SPREAD_AHEAD < CHUNKS_PER_SEQ:
                 spread_mask(r + SPREAD_AHEAD)
             for i in range(CHUNK // BLOCK):
                 if live(r + LOAD_AHEAD):
@@ -369,6 +377,9 @@ def tile_transformerencoderblock_pa_t_kernel(tc, h_attn, x, masks, Wo, bo, out):
             for half in range(HALVES):
                 if live(r - LAG * half + RESIDUAL_AHEAD):
                     load_residual(r - LAG * half + RESIDUAL_AHEAD, half)
+            seq, j = divmod(r + MASK_AHEAD, CHUNKS_PER_SEQ)
+            if 0 < seq < SEQS and j == 0:
+                load_mask(seq)
             for half in range(HALVES):
                 if live(r - LAG * half):
                     add_bias_and_mask(r - LAG * half, half)

@@ -36,7 +36,7 @@ NORM_BEHIND = CHUNKS_PER_SEQ + 1
 RESIDUAL_AHEAD = 2
 
 QUARTER = FRAMES // 4
-NORM_GPSIMD_COLS = 3 * NORM_PART // 4
+NORM_GPSIMD_COLS = 5 * NORM_PART // 8
 HALF_WINDOW_COLS = NORM_GPSIMD_COLS // 2
 
 

from contextlib import ExitStack

import concourse.mybir as mybir
from concourse.masks import make_identity

F32 = mybir.dt.float32
BF16 = mybir.dt.bfloat16
U32 = mybir.dt.uint32
U8 = mybir.dt.uint8
FP8X4 = mybir.dt.float8_e4m3fn_x4
ALU = mybir.AluOpType
ACT = mybir.ActivationFunctionType

P = 128
SEQS, FRAMES, C_IN, C_OUT = 3, 4096, 512, 256
EPS = 1e-5
FLOPS = 2 * SEQS * FRAMES * C_IN * C_OUT

WORDS = C_IN // 2
BLOCK = 512
ROWS = BLOCK // P
CHUNK = 2 * BLOCK
CHUNKS_PER_SEQ = FRAMES // CHUNK
CHUNKS = SEQS * CHUNKS_PER_SEQ
HALVES = C_OUT // P
NORM_PART = 2 * CHUNK

LAG = 2
LOAD_AHEAD = 4
FLIP_AHEAD = 2
SPREAD_AHEAD = 1
MASK_AHEAD = 3
MULTIPLY_AHEAD = 1
SQUARES_BEHIND = 1
NORM_BEHIND = CHUNKS_PER_SEQ + 1
RESIDUAL_AHEAD = 2

QUARTER = FRAMES // 4
NORM_GPSIMD_COLS = 5 * NORM_PART // 8
HALF_WINDOW_COLS = NORM_GPSIMD_COLS // 2


def tile_transformerencoderblock_pa_t_kernel(tc, h_attn, x, masks, Wo, bo, out):
    nc = tc.nc
    with ExitStack() as ctx:
        const = ctx.enter_context(tc.tile_pool(name="const", bufs=1))
        blocks_in = ctx.enter_context(tc.tile_pool(name="blocks_in", bufs=2 * LOAD_AHEAD))
        steps_in = ctx.enter_context(tc.tile_pool(name="steps_in", bufs=HALVES * (RESIDUAL_AHEAD + 1)))
        masks_in = ctx.enter_context(tc.tile_pool(name="masks_in", bufs=SEQS))
        stage = ctx.enter_context(tc.tile_pool(name="stage", bufs=4))
        per_chunk = ctx.enter_context(tc.tile_pool(name="per_chunk", bufs=FLIP_AHEAD + LAG))
        per_group = ctx.enter_context(tc.tile_pool(name="per_group", bufs=4))
        psum = ctx.enter_context(tc.psum_pool(name="psum", bufs=1))
        ctx.enter_context(tc.manual_schedule())

        ident_f32 = const.tile([P, P], F32)
        make_identity(nc, ident_f32[:])

        last_code = const.tile([P, 1], U32)
        last_sum = const.tile([P, 1], F32)

        raw, grouped = {}, {}
        codes, scales, mask_rows = {}, {}, {}
        product = {}
        residual, y, sums, neg_pivot, neg_mean, off_sq, affine = {}, {}, {}, {}, {}, {}, {}
        chores = []

        def add_chore(group, chore):
            chores.append((group, chore))

        def do_chore():
            if chores:
                chores.pop(0)[1]()

        def finish_chores(group):
            while any(waiting[0] == group for waiting in chores):
                do_chore()

        def flip_two(rows_words, grouped_words, by_vector):
            bank = psum.tile([P, 2, 2, P], F32, tag="flip", bufs=3)
            for row_block in range(2):
                for odd in range(2):
                    words = rows_words[:, WORDS * row_block + odd : WORDS * (row_block + 1) : 2]
                    nc.tensor.transpose(bank[:, row_block, odd, :], words, ident_f32[:])
            dst = grouped_words.rearrange("w (b r u) -> w b r u", b=2, u=2)
            src = bank[:].rearrange("w b u r -> w b r u")
            if by_vector:
                nc.vector.tensor_copy(out=dst, in_=src)
            else:
                nc.scalar.copy(out=dst, in_=src)
                do_chore()

        small_rows = const.tile([P, 2 * P], BF16)
        nc.vector.memset(small_rows[:], 0.0)
        one = const.tile([P, 2], F32)
        nc.vector.memset(one[:], 1.0)
        mask_row_count = SEQS * FRAMES // (2 * P)
        nc.scalar.dma_start(
            out=small_rows[0:mask_row_count, :], in_=masks.rearrange("n o (i r) -> (n o i) r", r=2 * P)
        )
        nc.scalar.dma_start(
            out=small_rows[mask_row_count : mask_row_count + 1, :], in_=bo.rearrange("(o c) -> o c", o=1)
        )
        w_raw = const.tile([P, HALVES * C_IN], BF16)
        def load_weights():
            nc.sync.dma_start(out=w_raw[:], in_=Wo.rearrange("(p h) k -> p (h k)", h=HALVES))

        nc.scalar.activation(out=one[:, 1:2], in_=one[:, 0:1], func=ACT.Abs_reciprocal_sqrt)
        mask_words = const.tile([P, mask_row_count], F32)
        bias_cols = const.tile([P, HALVES], F32)
        w_grouped = const.tile([P, HALVES * C_IN], BF16, align_bytes=64)
        w_codes = const.tile([P, C_OUT], U32, align_bytes=64)
        w_scales = const.tile([P, C_OUT], U8, align_bytes=64)

        def prepare_small_inputs():
            small_cols = psum.tile([P, CHUNK // 2], F32, tag="spread", bufs=1)
            nc.tensor.transpose(small_cols[:, 0:P], small_rows[:].bitcast(F32), ident_f32[:])
            nc.vector.tensor_copy(out=mask_words[:], in_=small_cols[:, 0:mask_row_count])
            nc.vector.tensor_copy(
                out=bias_cols[:], in_=small_cols[:, mask_row_count : mask_row_count + 1].bitcast(BF16)
            )
        def flip_weights():
            flip_two(w_raw[:].bitcast(F32), w_grouped[:].bitcast(F32), True)

        def quantise_weights():
            nc.vector.quantize_mx(out=w_codes[:].bitcast(FP8X4), scales=w_scales[:], in_=w_grouped[:])

        x_halves = x.rearrange("n (p h) t -> n h p t", h=HALVES)
        out_halves = out.rearrange("n (p h) t -> n h p t", h=HALVES)

        def load_block(chunk, i, pieces=1):
            seq, j = divmod(chunk, CHUNKS_PER_SEQ)
            first = CHUNK * j + BLOCK * i
            raw[(chunk, i)] = blocks_in.tile([P, ROWS * C_IN], BF16, name="raw")
            rows = h_attn[seq, first : first + BLOCK, :].rearrange("(p a) k -> p (a k)", a=ROWS)
            width = ROWS * C_IN // pieces
            for piece in range(pieces):
                cols = slice(width * piece, width * (piece + 1))
                nc.sync.dma_start(out=raw[(chunk, i)][:, cols], in_=rows[:, cols])

        def load_residual(chunk, half):
            seq, j = divmod(chunk, CHUNKS_PER_SEQ)
            cols = slice(CHUNK * j, CHUNK * (j + 1))
            residual[(chunk, half)] = steps_in.tile([P, CHUNK], BF16, name="residual")
            nc.sync.dma_start(out=residual[(chunk, half)][:], in_=x_halves[seq, half, :, cols])

        def flip_block(chunk, i, by_vector=()):
            grouped[(chunk, i)] = stage.tile([P, 4 * BLOCK], BF16, name="grouped", align_bytes=64)
            raw_words = raw[(chunk, i)][:].bitcast(F32)
            grouped_words = grouped[(chunk, i)][:].bitcast(F32)
            for pair in range(ROWS // 2):
                cols = slice(2 * WORDS * pair, 2 * WORDS * (pair + 1))
                flip_two(raw_words[:, cols], grouped_words[:, cols], pair in by_vector)

        def load_mask(seq):
            mask_rows[seq] = masks_in.tile([P, FRAMES], BF16, name="mask_rows")
            nc.sync.dma_start(out=mask_rows[seq][:], in_=masks[seq, 0, :].partition_broadcast(P))

        def spread_mask(chunk):
            if chunk == 0:
                mask_rows[0] = masks_in.tile([P, FRAMES], BF16, name="mask_rows")
            spread = psum.tile([P, CHUNK // 2], F32, tag="spread", bufs=1)
            for i in range(CHUNK // (2 * P)):
                col = CHUNK // (2 * P) * chunk + i
                nc.tensor.transpose(
                    spread[:, P * i : P * (i + 1)],
                    mask_words[:, col : col + 1].to_broadcast([P, P]),
                    ident_f32[:],
                )
            nc.scalar.copy(
                out=mask_rows[0][:, CHUNK * chunk : CHUNK * (chunk + 1)], in_=spread[:].bitcast(BF16)
            )
            do_chore()

        def quantise_block(chunk, i):
            if i == 0:
                codes[chunk] = per_chunk.tile([P, CHUNK], U32, name="codes", align_bytes=64)
                scales[chunk] = per_chunk.tile([P, CHUNK], U8, name="scales", align_bytes=64)
            cols = slice(BLOCK * i, BLOCK * (i + 1))
            nc.vector.quantize_mx(
                out=codes[chunk][:, cols].bitcast(FP8X4),
                scales=scales[chunk][:, cols],
                in_=grouped[(chunk, i)][:],
            )

        def multiply(chunk, half):
            for i in range(CHUNK // BLOCK):
                cols = slice(BLOCK * i, BLOCK * (i + 1))
                product[(chunk, half, i)] = psum.tile([P, BLOCK], F32, tag="product", bufs=4, name="product")
                nc.tensor.matmul_mx(
                    out=product[(chunk, half, i)][:],
                    lhsT=w_codes[:, P * half : P * (half + 1)].bitcast(FP8X4),
                    lhsT_scale=w_scales[:, P * half : P * (half + 1)],
                    rhs=codes[chunk][:, cols].bitcast(FP8X4),
                    rhs_scale=scales[chunk][:, cols],
                    start=True,
                    stop=True,
                )

        def add_bias_and_mask(chunk, half):
            seq, j = divmod(chunk, CHUNKS_PER_SEQ)
            group = (seq, half)
            if j == 0:
                y[group] = per_group.tile([P, FRAMES], F32, name="y")
                sums[group] = per_group.tile([P, 2, 8], F32, name="sums")
            for i in range(CHUNK // BLOCK):
                first = CHUNK * j + BLOCK * i
                nc.vector.scalar_tensor_tensor(
                    out=y[group][:, first : first + BLOCK].rearrange("e (p a) -> e p a", a=ROWS),
                    in0=product[(chunk, half, i)][:].rearrange("e (a p) -> e p a", a=ROWS),
                    scalar=bias_cols[:, half : half + 1],
                    in1=mask_rows[seq][:, first : first + BLOCK].rearrange("e (p a) -> e p a", a=ROWS),
                    op0=ALU.add,
                    op1=ALU.mult,
                )

        def add_residual(chunk, half, pieces=1):
            seq, j = divmod(chunk, CHUNKS_PER_SEQ)
            for piece in range(pieces):
                add_residual_piece(
                    (seq, half), j, residual[(chunk, half)], CHUNK // pieces * piece, CHUNK // pieces, j + piece
                )
            if j == CHUNKS_PER_SEQ - 1:
                early_statistics((seq, half), CHUNKS_PER_SEQ - 1 + pieces)

        def add_residual_piece(group, j, x_step, first, width, sum_col):
            cols = slice(CHUNK * j + first, CHUNK * j + first + width)
            nc.vector.scalar_tensor_tensor(
                out=y[group][:, cols],
                in0=y[group][:, cols],
                scalar=1.0,
                in1=x_step[:, first : first + width],
                op0=ALU.mult,
                op1=ALU.add,
                accum_out=sums[group][:, 0, sum_col : sum_col + 1],
            )
            if j == 0:
                neg_pivot[group] = per_group.tile([P, 1], F32, name="neg_pivot")
                add_chore(
                    group,
                    lambda: nc.scalar.activation(
                        out=neg_pivot[group][:], in_=sums[group][:, 0, 0:1], func=ACT.Identity, scale=-1.0 / CHUNK
                    )
                )
        def sum_squares(chunk, half, pieces=1):
            seq, j = divmod(chunk, CHUNKS_PER_SEQ)
            group = (seq, half)
            if j == 0:
                finish_chores(group)
            width = CHUNK // pieces
            for piece in range(pieces):
                first = CHUNK * j + width * piece
                squares = stage.tile([P, CHUNK], BF16, name="squares")
                nc.scalar.activation(
                    out=squares[:, 0:width], in_=y[group][:, first : first + width], func=ACT.Square,
                    bias=neg_pivot[group][:, 0:1], accum_out=sums[group][:, 1, j + piece : j + piece + 1],
                )
                do_chore()
            if j == CHUNKS_PER_SEQ - 1:
                late_statistics(group, CHUNKS_PER_SEQ - 1 + pieces)

        def early_statistics(group, count):
            neg_mean[group] = per_group.tile([P, 1], F32, name="neg_mean")
            off_sq[group] = per_group.tile([P, 1], F32, name="off_sq")
            terms = per_group.tile([P, 8], F32, name="terms")
            add_chore(
                group,
                lambda: nc.scalar.activation(
                    out=terms[:, 0:count], in_=sums[group][:, 0, 0:count], func=ACT.Identity,
                    scale=-1.0 / FRAMES, accum_out=neg_mean[group][:],
                )
            )
            add_chore(
                group,
                lambda: nc.scalar.activation(
                    out=off_sq[group][:], in_=neg_mean[group][:], func=ACT.Square,
                    bias=neg_pivot[group][:], scale=-1.0,
                )
            )

        def late_statistics(group, count):
            square_eps = per_group.tile([P, 1], F32, name="square_eps")
            terms = per_group.tile([P, 8], F32, name="terms")
            affine[group] = per_group.tile([P, 2], F32, name="affine")
            add_chore(
                group,
                lambda: nc.scalar.activation(
                    out=terms[:, 0:count], in_=sums[group][:, 1, 0:count], func=ACT.Identity,
                    bias=EPS / count, scale=1.0 / FRAMES, accum_out=square_eps[:],
                )
            )
            add_chore(
                group,
                lambda: nc.scalar.activation(
                    out=affine[group][:, 0:1], in_=off_sq[group][:], func=ACT.Abs_reciprocal_sqrt,
                    bias=square_eps[:], scale=-1.0,
                )
            )
            add_chore(
                group,
                lambda: nc.scalar.activation(
                    out=affine[group][:, 1:2], in_=neg_mean[group][:], func=ACT.Identity, scale=affine[group][:, 0:1]
                )
            )

        def hold_gpsimd(copy_of, written_last):
            nc.gpsimd.tensor_copy(out=copy_of[:], in_=written_last)

        def normalise(group, first, last, engine):
            finish_chores(group)
            cols = y[group][:, first:last]
            if engine == "gpsimd":
                nc.gpsimd.tensor_scalar(
                    out=cols, in0=cols, scalar1=affine[group][:, 0:1], scalar2=affine[group][:, 1:2], op0=ALU.mult, op1=ALU.add
                )
            elif engine == "vector":
                nc.vector.tensor_scalar(
                    out=cols, in0=cols, scalar1=neg_mean[group][:, 0:1], scalar2=affine[group][:, 0:1],
                    op0=ALU.add, op1=ALU.mult,
                )
            else:
                nc.scalar.activation(
                    out=cols, in_=cols, func=ACT.Identity, bias=affine[group][:, 1:2], scale=affine[group][:, 0:1]
                )

        def parts_of_round(r):
            for half in range(HALVES):
                seq, part = divmod(r - LAG * half - NORM_BEHIND, CHUNKS_PER_SEQ)
                if 0 <= seq < SEQS and part < FRAMES // NORM_PART:
                    return [((seq, half), part)]
            return []

        def store(group, first, last):
            seq, half = group
            nc.sync.dma_start(out=out_halves[seq, half, :, first:last], in_=y[group][:, first:last])

        def live(chunk):
            return 0 <= chunk < CHUNKS

        load_block(0, 0, 2)
        load_weights()
        load_block(0, 1, 2)
        for i in range(CHUNK // BLOCK):
            load_block(1, i, 2)
        load_residual(0, 0)
        for i in range(CHUNK // BLOCK):
            load_block(2, i)
        load_residual(1, 0)
        for i in range(CHUNK // BLOCK):
            load_block(3, i)
        flip_block(0, 0)
        flip_weights()
        prepare_small_inputs()
        flip_block(0, 1)
        quantise_block(0, 0)
        quantise_weights()
        quantise_block(0, 1)
        spread_mask(0)
        flip_block(1, 0)
        multiply(0, 0)
        flip_block(1, 1)

        squared_late = [(CHUNKS - 1, 0), (CHUNKS - LAG - 1, 1), (CHUNKS - LAG, 1), (CHUNKS - 1, 1)]
        for r in range(CHUNKS + LAG):
            for half in range(HALVES):
                chunk = r - LAG * half - SQUARES_BEHIND
                if live(chunk) and (chunk, half) not in squared_late:
                    sum_squares(chunk, half)
            for i in range(CHUNK // BLOCK):
                if live(r + FLIP_AHEAD):
                    flip_block(r + FLIP_AHEAD, i)
            if r + SPREAD_AHEAD < CHUNKS_PER_SEQ:
                spread_mask(r + SPREAD_AHEAD)
            for i in range(CHUNK // BLOCK):
                if live(r + LOAD_AHEAD):
                    load_block(r + LOAD_AHEAD, i)
            for half in range(HALVES):
                if live(r - LAG * half + RESIDUAL_AHEAD):
                    load_residual(r - LAG * half + RESIDUAL_AHEAD, half)
            seq, j = divmod(r + MASK_AHEAD, CHUNKS_PER_SEQ)
            if 0 < seq < SEQS and j == 0:
                load_mask(seq)
            for half in range(HALVES):
                if live(r - LAG * half):
                    add_bias_and_mask(r - LAG * half, half)
            if r == 0:
                quantise_block(1, 0)
                quantise_block(1, 1)
            for half in range(HALVES):
                if live(r - LAG * half + MULTIPLY_AHEAD):
                    multiply(r - LAG * half + MULTIPLY_AHEAD, half)
            if r == CHUNKS:
                normalise((2, 0), 0, QUARTER, "vector")
                store((2, 0), 0, QUARTER)
            for half in range(HALVES):
                if live(r - LAG * half):
                    add_residual(r - LAG * half, half, 2 if r == CHUNKS + LAG - 1 else 1)
                if live(r + FLIP_AHEAD):
                    quantise_block(r + FLIP_AHEAD, half)
            if r < CHUNKS:
                for group, part in parts_of_round(r):
                    first, last = NORM_PART * part, NORM_PART * (part + 1)
                    if group == (1, 1):
                        first, last = QUARTER, 3 * QUARTER
                    normalise(group, first, first + NORM_GPSIMD_COLS, "gpsimd")
                    normalise(group, first + NORM_GPSIMD_COLS, last, "scalar")
                    store(group, first, last)
            if r == CHUNKS - 2:
                normalise((1, 1), 0, QUARTER, "scalar")
                store((1, 1), 0, QUARTER)
            if r == CHUNKS - 1:
                do_chore()
                sum_squares(CHUNKS - 1, 0)
                finish_chores((2, 0))
            if r == CHUNKS:
                normalise((1, 1), 3 * QUARTER, 3 * QUARTER + HALF_WINDOW_COLS, "gpsimd")
                normalise((1, 1), 3 * QUARTER + HALF_WINDOW_COLS, FRAMES, "scalar")
                store((1, 1), 3 * QUARTER, FRAMES)
                normalise((2, 0), QUARTER, 2 * QUARTER, "scalar")
                store((2, 0), QUARTER, 2 * QUARTER)
                sum_squares(CHUNKS - LAG - 1, 1)
                sum_squares(CHUNKS - LAG, 1)
            if r == CHUNKS + 1:
                normalise((2, 0), 3 * QUARTER, 3 * QUARTER + HALF_WINDOW_COLS, "gpsimd")
                normalise((2, 0), 3 * QUARTER + HALF_WINDOW_COLS, FRAMES, "scalar")
                store((2, 0), 3 * QUARTER, FRAMES)
                sum_squares(CHUNKS - 1, 1, 2)
                normalise((2, 0), 2 * QUARTER, 3 * QUARTER, "vector")
                store((2, 0), 2 * QUARTER, 3 * QUARTER)
            if r >= NORM_BEHIND - 1:
                if live(r + FLIP_AHEAD):
                    hold_gpsimd(last_code, codes[r + FLIP_AHEAD][:, CHUNK - 1 : CHUNK])
                elif live(r - LAG):
                    seq, j = divmod(r - LAG, CHUNKS_PER_SEQ)
                    hold_gpsimd(last_sum, sums[(seq, 1)][:, 0, j : j + 1])

        for first, last in ((0, BLOCK), (BLOCK, QUARTER), (QUARTER, 2 * QUARTER), (2 * QUARTER, FRAMES)):
            normalise((2, 1), first, last, "vector")
            store((2, 1), first, last)
